import numpy as np
import ml_dtypes


def mxq(x, axis, fmt="e4m3"):
    dtype, down = {"e4m3": (ml_dtypes.float8_e4m3fn, 7), "e5m2": (ml_dtypes.float8_e5m2, 14)}[fmt]
    v = np.moveaxis(np.asarray(x, np.float32).astype(ml_dtypes.bfloat16).astype(np.float64), axis, -1)
    blocks = v.reshape(v.shape[:-1] + (-1, 32))
    amax = np.abs(blocks).max(-1, keepdims=True)
    byte = np.maximum(np.where(amax > 0, np.frexp(amax)[1] - 1 + 127, 0) - down, 1)
    scale = np.exp2(byte - 127.0)
    codes = (blocks / scale).astype(np.float32).astype(dtype).astype(np.float64)
    return np.moveaxis((codes * scale).reshape(v.shape), -1, axis)


WIDE = False


def mx_kscale(k):
    if not WIDE:
        return np.ones(k)
    levels = np.array([10, -10, 5, -5, 0])
    a = np.random.permutation(np.resize(levels, k // 512 * 4)).reshape(k // 512, 4)
    idx = np.arange(k)
    return np.exp2(a[idx // 512, idx % 128 // 32])


BF16 = ml_dtypes.bfloat16


def bf(x):
    return np.asarray(x, np.float32).astype(BF16)


def f64(x):
    return np.asarray(x).astype(np.float64)


B, H, L, E, QD = 64, 1, 128, 1024, 128


def setup_inputs():
    s = mx_kscale(E)
    return {"x": bf(np.random.standard_normal((B, H, L, E)) * s),
            "Wk": bf(np.random.standard_normal((QD, E)) * 0.3 / np.sqrt(E) / s),
            "bk": bf(0.1 + 0.1 * np.random.standard_normal(QD)),
            "Wv": bf(np.random.standard_normal((QD, E)) * 0.3 / np.sqrt(E) / s),
            "bv": bf(0.1 + 0.1 * np.random.standard_normal(QD))}


def reference(x, Wk, bk, Wv, bv):
    xq = mxq(f64(x), 3, "e4m3")
    K = (xq @ mxq(f64(Wk), 1, "e4m3").T) + f64(bk)
    V = (xq @ mxq(f64(Wv), 1, "e4m3").T) + f64(bv)
    return K * V

@@ -1,0 +1,165 @@
+from contextlib import ExitStack
+
+import concourse.mybir as mybir
+from concourse.masks import make_identity
+
+BF16 = mybir.dt.bfloat16
+F32 = mybir.dt.float32
+U32 = mybir.dt.uint32
+U8 = mybir.dt.uint8
+FP8X4 = mybir.dt.float8_e4m3fn_x4
+ADD = mybir.AluOpType.add
+MULT = mybir.AluOpType.mult
+
+P = 128
+ROWS = 64 * 128
+K = 1024
+QD = 128
+PACK = 4
+PASSES = K // (P * PACK)
+WORDS = K // 2
+BLOCKS = WORDS // P
+BOTH = 2 * QD
+TILES = 4
+CHUNKS = ROWS // (P * TILES)
+PAIRS = TILES // 2
+X_BUFS = 8
+OUT_BUFS = 8
+
+FLOPS = 2 * ROWS * K * BOTH
+
+
+def tile_parallelretention_pa_t_kernel(tc, x, Wk, bk, Wv, bv, out):
+    nc = tc.nc
+    x_chunks = x.flatten_outer_dims().rearrange("(p c j) k -> c p (j k)", p=P, c=CHUNKS, j=TILES)
+    out_chunks = out.flatten_outer_dims().rearrange("(p c j) q -> c p (j q)", p=P, c=CHUNKS, j=TILES)
+
+    with ExitStack() as ctx:
+        ctx.enter_context(tc.manual_schedule())
+        const = ctx.enter_context(tc.tile_pool(name="const", bufs=1))
+        x_pool = ctx.enter_context(tc.tile_pool(name="x_pool", bufs=X_BUFS))
+        mx_pool = ctx.enter_context(tc.tile_pool(name="mx_pool", bufs=3))
+        out_pool = ctx.enter_context(tc.tile_pool(name="out_pool", bufs=OUT_BUFS))
+        turned_pool = ctx.enter_context(tc.psum_pool(name="turned_pool", bufs=TILES))
+        sums_pool = ctx.enter_context(tc.psum_pool(name="sums_pool", bufs=2 * PAIRS))
+
+        def load_chunk(c):
+            x_rows = x_pool.tile([P, TILES * K], BF16, name="x_rows")
+            nc.sync.dma_start(out=x_rows[:], in_=x_chunks[c])
+            return x_rows
+
+        def turn_row_tile(row_words, grouped_words):
+            turned = turned_pool.tile([P, WORDS], F32, name="turned")
+            for b in range(BLOCKS):
+                cols = slice(b * P, (b + 1) * P)
+                nc.tensor.transpose(out=turned[:, cols], in_=row_words[:, cols], identity=identity[:])
+            nc.scalar.copy(
+                out=grouped_words,
+                in_=turned[:].rearrange("p (g u r) -> p g r u", g=PASSES, u=2),
+            )
+
+        w_rows = const.tile([P, 2 * K], BF16, name="w_rows")
+        nc.sync.dma_start(out=w_rows[:, 0:K], in_=Wk)
+        nc.sync.dma_start(out=w_rows[:, K : 2 * K], in_=Wv)
+        x_tiles = {}
+        for c in range(X_BUFS):
+            x_tiles[c] = load_chunk(c)
+
+        identity = const.tile([P, P], F32, name="identity")
+        make_identity(nc, identity[:])
+
+        bias_rows = const.tile([P, BOTH], BF16, name="bias_rows")
+        nc.vector.memset(bias_rows[:], 0.0)
+        nc.scalar.dma_start(out=bias_rows[0:1, 0:QD], in_=bk.rearrange("(o q) -> o q", o=1))
+        nc.scalar.dma_start(out=bias_rows[0:1, QD:BOTH], in_=bv.rearrange("(o q) -> o q", o=1))
+        ones = const.tile([P, P], BF16, name="ones")
+        nc.vector.memset(ones[:], 1.0)
+        bias_sums = sums_pool.tile([P, 2 * BOTH], F32, name="sums")
+        nc.tensor.matmul(out=bias_sums[:, 0:BOTH], lhsT=ones[:], rhs=bias_rows[:], start=True, stop=True)
+        bias = const.tile([P, BOTH], F32, name="bias")
+        nc.vector.tensor_copy(out=bias[:], in_=bias_sums[:, 0:BOTH])
+
+        w_grouped = const.tile([P, PASSES * BOTH * PACK], BF16, name="w_grouped", align_bytes=64)
+        w_codes = const.tile([P, PASSES * BOTH], U32, name="w_codes", align_bytes=64)
+        w_scales = const.tile([P, PASSES * BOTH], U8, name="w_scales", align_bytes=64)
+        w_words = w_rows[:].bitcast(F32)
+        w_grouped_words = w_grouped[:].bitcast(F32).rearrange("p (g v r u) -> p g v r u", g=PASSES, v=2, u=2)
+        for v in range(2):
+            turn_row_tile(w_words[:, v * WORDS : (v + 1) * WORDS], w_grouped_words[:, :, v, :, :])
+        nc.vector.quantize_mx(out=w_codes[:].bitcast(FP8X4), scales=w_scales[:], in_=w_grouped[:])
+
+        grouped_tiles = {}
+        code_tiles = {}
+        scale_tiles = {}
+        sum_tiles = {}
+        biased_tiles = {}
+
+        def turn_chunk(c):
+            grouped_tiles[c] = mx_pool.tile([P, TILES * K], BF16, name="grouped", align_bytes=64)
+            code_tiles[c] = mx_pool.tile([P, TILES * K // PACK], U32, name="codes", align_bytes=64)
+            scale_tiles[c] = mx_pool.tile([P, TILES * K // PACK], U8, name="scales", align_bytes=64)
+            x_words = x_tiles[c][:].bitcast(F32)
+            grouped_words = grouped_tiles[c][:].bitcast(F32)
+            for j in range(TILES):
+                words = slice(j * WORDS, (j + 1) * WORDS)
+                turn_row_tile(
+                    x_words[:, words],
+                    grouped_words[:, words].rearrange("p (g r u) -> p g r u", g=PASSES, u=2),
+                )
+
+        def quantise_pair(c, h):
+            width = 2 * K // PACK
+            nc.vector.quantize_mx(
+                out=code_tiles[c][:, h * width : (h + 1) * width].bitcast(FP8X4),
+                scales=scale_tiles[c][:, h * width : (h + 1) * width],
+                in_=grouped_tiles[c][:, h * width * PACK : (h + 1) * width * PACK],
+            )
+
+        def multiply_chunk(c):
+            for h in range(PAIRS):
+                sums = sums_pool.tile([P, 2 * BOTH], F32, name="sums")
+                sum_tiles[c, h] = sums
+                for i in range(2):
+                    for g in range(PASSES):
+                        first = ((2 * h + i) * PASSES + g) * P
+                        nc.tensor.matmul_mx(
+                            out=sums[:, i * BOTH : (i + 1) * BOTH],
+                            lhsT=code_tiles[c][:, first : first + P].bitcast(FP8X4),
+                            lhsT_scale=scale_tiles[c][:, first : first + P],
+                            rhs=w_codes[:, g * BOTH : (g + 1) * BOTH].bitcast(FP8X4),
+                            rhs_scale=w_scales[:, g * BOTH : (g + 1) * BOTH],
+                            start=(g == 0),
+                            stop=(g == PASSES - 1),
+                        )
+
+        def add_bias_pair(c, h):
+            if h == 0:
+                biased_tiles[c] = mx_pool.tile([P, TILES, BOTH], F32, name="biased")
+            nc.vector.tensor_tensor(
+                out=biased_tiles[c][:, 2 * h : 2 * h + 2, :],
+                in0=sum_tiles[c, h][:].rearrange("p (i n) -> p i n", i=2),
+                in1=bias[:].unsqueeze(1).to_broadcast([P, 2, BOTH]),
+                op=ADD,
+            )
+
+        def finish_chunk(c):
+            kv = out_pool.tile([P, TILES, QD], F32, name="kv")
+            nc.vector.tensor_tensor(
+                out=kv[:], in0=biased_tiles[c][:, :, 0:QD], in1=biased_tiles[c][:, :, QD:BOTH], op=MULT
+            )
+            nc.sync.dma_start(out=out_chunks[c], in_=kv[:].rearrange("p j q -> p (j q)"))
+
+        turn_chunk(0)
+        for h in range(PAIRS):
+            quantise_pair(0, h)
+        for c in range(1, CHUNKS + 1):
+            if c - 1 + X_BUFS < CHUNKS:
+                x_tiles[c - 1 + X_BUFS] = load_chunk(c - 1 + X_BUFS)
+            if c < CHUNKS:
+                turn_chunk(c)
+            multiply_chunk(c - 1)
+            for h in range(PAIRS):
+                if c < CHUNKS:
+                    quantise_pair(c, h)
+                add_bias_pair(c - 1, h)
+            finish_chunk(c - 1)

@@ -58,13 +58,6 @@ def tile_parallelretention_pa_t_kernel(tc, x, Wk, bk, Wv, bv, out):
                 in_=turned[:].rearrange("p (g u r) -> p g r u", g=PASSES, u=2),
             )
 
-        w_rows = const.tile([P, 2 * K], BF16, name="w_rows")
-        nc.sync.dma_start(out=w_rows[:, 0:K], in_=Wk)
-        nc.sync.dma_start(out=w_rows[:, K : 2 * K], in_=Wv)
-        x_tiles = {}
-        for c in range(X_BUFS):
-            x_tiles[c] = load_chunk(c)
-
         identity = const.tile([P, P], F32, name="identity")
         make_identity(nc, identity[:])
 
@@ -74,19 +67,13 @@ def tile_parallelretention_pa_t_kernel(tc, x, Wk, bk, Wv, bv, out):
         nc.scalar.dma_start(out=bias_rows[0:1, QD:BOTH], in_=bv.rearrange("(o q) -> o q", o=1))
         ones = const.tile([P, P], BF16, name="ones")
         nc.vector.memset(ones[:], 1.0)
-        bias_sums = sums_pool.tile([P, 2 * BOTH], F32, name="sums")
-        nc.tensor.matmul(out=bias_sums[:, 0:BOTH], lhsT=ones[:], rhs=bias_rows[:], start=True, stop=True)
-        bias = const.tile([P, BOTH], F32, name="bias")
-        nc.vector.tensor_copy(out=bias[:], in_=bias_sums[:, 0:BOTH])
 
-        w_grouped = const.tile([P, PASSES * BOTH * PACK], BF16, name="w_grouped", align_bytes=64)
-        w_codes = const.tile([P, PASSES * BOTH], U32, name="w_codes", align_bytes=64)
-        w_scales = const.tile([P, PASSES * BOTH], U8, name="w_scales", align_bytes=64)
-        w_words = w_rows[:].bitcast(F32)
-        w_grouped_words = w_grouped[:].bitcast(F32).rearrange("p (g v r u) -> p g v r u", g=PASSES, v=2, u=2)
-        for v in range(2):
-            turn_row_tile(w_words[:, v * WORDS : (v + 1) * WORDS], w_grouped_words[:, :, v, :, :])
-        nc.vector.quantize_mx(out=w_codes[:].bitcast(FP8X4), scales=w_scales[:], in_=w_grouped[:])
+        x_tiles = {0: load_chunk(0)}
+        w_rows = const.tile([P, 2 * K], BF16, name="w_rows")
+        nc.sync.dma_start(out=w_rows[:, 0:K], in_=Wk)
+        nc.sync.dma_start(out=w_rows[:, K : 2 * K], in_=Wv)
+        for c in range(1, X_BUFS):
+            x_tiles[c] = load_chunk(c)
 
         grouped_tiles = {}
         code_tiles = {}
@@ -152,6 +139,21 @@ def tile_parallelretention_pa_t_kernel(tc, x, Wk, bk, Wv, bv, out):
         turn_chunk(0)
         for h in range(PAIRS):
             quantise_pair(0, h)
+
+        w_grouped = const.tile([P, PASSES * BOTH * PACK], BF16, name="w_grouped", align_bytes=64)
+        w_codes = const.tile([P, PASSES * BOTH], U32, name="w_codes", align_bytes=64)
+        w_scales = const.tile([P, PASSES * BOTH], U8, name="w_scales", align_bytes=64)
+        w_words = w_rows[:].bitcast(F32)
+        w_grouped_words = w_grouped[:].bitcast(F32).rearrange("p (g v r u) -> p g v r u", g=PASSES, v=2, u=2)
+        for v in range(2):
+            turn_row_tile(w_words[:, v * WORDS : (v + 1) * WORDS], w_grouped_words[:, :, v, :, :])
+        nc.vector.quantize_mx(out=w_codes[:].bitcast(FP8X4), scales=w_scales[:], in_=w_grouped[:])
+
+        bias_sums = sums_pool.tile([P, 2 * BOTH], F32, name="sums")
+        nc.tensor.matmul(out=bias_sums[:, 0:BOTH], lhsT=ones[:], rhs=bias_rows[:], start=True, stop=True)
+        bias = const.tile([P, BOTH], F32, name="bias")
+        nc.vector.tensor_copy(out=bias[:], in_=bias_sums[:, 0:BOTH])
+
         for c in range(1, CHUNKS + 1):
             if c - 1 + X_BUFS < CHUNKS:
                 x_tiles[c - 1 + X_BUFS] = load_chunk(c - 1 + X_BUFS)

@@ -23,7 +23,7 @@ BOTH = 2 * QD
 TILES = 4
 CHUNKS = ROWS // (P * TILES)
 PAIRS = TILES // 2
-X_BUFS = 8
+AHEAD = 8
 OUT_BUFS = 8
 
 FLOPS = 2 * ROWS * K * BOTH
@@ -31,22 +31,24 @@ FLOPS = 2 * ROWS * K * BOTH
 
 def tile_parallelretention_pa_t_kernel(tc, x, Wk, bk, Wv, bv, out):
     nc = tc.nc
-    x_chunks = x.flatten_outer_dims().rearrange("(p c j) k -> c p (j k)", p=P, c=CHUNKS, j=TILES)
-    out_chunks = out.flatten_outer_dims().rearrange("(p c j) q -> c p (j q)", p=P, c=CHUNKS, j=TILES)
+    x_pairs = x.flatten_outer_dims().rearrange("(c p h i) k -> c h p (i k)", c=CHUNKS, p=P, h=PAIRS, i=2)
+    out_chunks = out.flatten_outer_dims().rearrange("(c p j) q -> c p (j q)", c=CHUNKS, p=P, j=TILES)
 
     with ExitStack() as ctx:
         ctx.enter_context(tc.manual_schedule())
         const = ctx.enter_context(tc.tile_pool(name="const", bufs=1))
-        x_pool = ctx.enter_context(tc.tile_pool(name="x_pool", bufs=X_BUFS))
+        x_pool = ctx.enter_context(tc.tile_pool(name="x_pool", bufs=AHEAD * PAIRS))
         mx_pool = ctx.enter_context(tc.tile_pool(name="mx_pool", bufs=3))
         out_pool = ctx.enter_context(tc.tile_pool(name="out_pool", bufs=OUT_BUFS))
         turned_pool = ctx.enter_context(tc.psum_pool(name="turned_pool", bufs=TILES))
         sums_pool = ctx.enter_context(tc.psum_pool(name="sums_pool", bufs=2 * PAIRS))
 
+        x_tiles = {}
+
         def load_chunk(c):
-            x_rows = x_pool.tile([P, TILES * K], BF16, name="x_rows")
-            nc.sync.dma_start(out=x_rows[:], in_=x_chunks[c])
-            return x_rows
+            for h in range(PAIRS):
+                x_tiles[c, h] = x_pool.tile([P, 2 * K], BF16, name="x_rows")
+                nc.sync.dma_start(out=x_tiles[c, h][:], in_=x_pairs[c, h])
 
         def turn_row_tile(row_words, grouped_words):
             turned = turned_pool.tile([P, WORDS], F32, name="turned")
@@ -68,12 +70,12 @@ def tile_parallelretention_pa_t_kernel(tc, x, Wk, bk, Wv, bv, out):
         ones = const.tile([P, P], BF16, name="ones")
         nc.vector.memset(ones[:], 1.0)
 
-        x_tiles = {0: load_chunk(0)}
+        load_chunk(0)
         w_rows = const.tile([P, 2 * K], BF16, name="w_rows")
         nc.sync.dma_start(out=w_rows[:, 0:K], in_=Wk)
         nc.sync.dma_start(out=w_rows[:, K : 2 * K], in_=Wv)
-        for c in range(1, X_BUFS):
-            x_tiles[c] = load_chunk(c)
+        for c in range(1, AHEAD):
+            load_chunk(c)
 
         grouped_tiles = {}
         code_tiles = {}
@@ -85,13 +87,12 @@ def tile_parallelretention_pa_t_kernel(tc, x, Wk, bk, Wv, bv, out):
             grouped_tiles[c] = mx_pool.tile([P, TILES * K], BF16, name="grouped", align_bytes=64)
             code_tiles[c] = mx_pool.tile([P, TILES * K // PACK], U32, name="codes", align_bytes=64)
             scale_tiles[c] = mx_pool.tile([P, TILES * K // PACK], U8, name="scales", align_bytes=64)
-            x_words = x_tiles[c][:].bitcast(F32)
             grouped_words = grouped_tiles[c][:].bitcast(F32)
             for j in range(TILES):
-                words = slice(j * WORDS, (j + 1) * WORDS)
+                h, i = divmod(j, 2)
                 turn_row_tile(
-                    x_words[:, words],
-                    grouped_words[:, words].rearrange("p (g r u) -> p g r u", g=PASSES, u=2),
+                    x_tiles[c, h][:].bitcast(F32)[:, i * WORDS : (i + 1) * WORDS],
+                    grouped_words[:, j * WORDS : (j + 1) * WORDS].rearrange("p (g r u) -> p g r u", g=PASSES, u=2),
                 )
 
         def quantise_pair(c, h):
@@ -155,8 +156,8 @@ def tile_parallelretention_pa_t_kernel(tc, x, Wk, bk, Wv, bv, out):
         nc.vector.tensor_copy(out=bias[:], in_=bias_sums[:, 0:BOTH])
 
         for c in range(1, CHUNKS + 1):
-            if c - 1 + X_BUFS < CHUNKS:
-                x_tiles[c - 1 + X_BUFS] = load_chunk(c - 1 + X_BUFS)
+            if c - 1 + AHEAD < CHUNKS:
+                load_chunk(c - 1 + AHEAD)
             if c < CHUNKS:
                 turn_chunk(c)
             multiply_chunk(c - 1)

@@ -132,7 +132,7 @@ def tile_parallelretention_pa_t_kernel(tc, x, Wk, bk, Wv, bv, out):
 
         def finish_chunk(c):
             kv = out_pool.tile([P, TILES, QD], F32, name="kv")
-            nc.vector.tensor_tensor(
+            nc.gpsimd.tensor_tensor(
                 out=kv[:], in0=biased_tiles[c][:, :, 0:QD], in1=biased_tiles[c][:, :, QD:BOTH], op=MULT
             )
             nc.sync.dma_start(out=out_chunks[c], in_=kv[:].rearrange("p j q -> p (j q)"))

from contextlib import ExitStack

import concourse.mybir as mybir
from concourse.masks import make_identity

BF16 = mybir.dt.bfloat16
F32 = mybir.dt.float32
U32 = mybir.dt.uint32
U8 = mybir.dt.uint8
FP8X4 = mybir.dt.float8_e4m3fn_x4
ADD = mybir.AluOpType.add
MULT = mybir.AluOpType.mult

P = 128
ROWS = 64 * 128
K = 1024
QD = 128
PACK = 4
PASSES = K // (P * PACK)
WORDS = K // 2
BLOCKS = WORDS // P
BOTH = 2 * QD
TILES = 4
CHUNKS = ROWS // (P * TILES)
PAIRS = TILES // 2
AHEAD = 8
OUT_BUFS = 8

FLOPS = 2 * ROWS * K * BOTH


def tile_parallelretention_pa_t_kernel(tc, x, Wk, bk, Wv, bv, out):
    nc = tc.nc
    x_pairs = x.flatten_outer_dims().rearrange("(c p h i) k -> c h p (i k)", c=CHUNKS, p=P, h=PAIRS, i=2)
    out_chunks = out.flatten_outer_dims().rearrange("(c p j) q -> c p (j q)", c=CHUNKS, p=P, j=TILES)

    with ExitStack() as ctx:
        ctx.enter_context(tc.manual_schedule())
        const = ctx.enter_context(tc.tile_pool(name="const", bufs=1))
        x_pool = ctx.enter_context(tc.tile_pool(name="x_pool", bufs=AHEAD * PAIRS))
        mx_pool = ctx.enter_context(tc.tile_pool(name="mx_pool", bufs=3))
        out_pool = ctx.enter_context(tc.tile_pool(name="out_pool", bufs=OUT_BUFS))
        turned_pool = ctx.enter_context(tc.psum_pool(name="turned_pool", bufs=TILES))
        sums_pool = ctx.enter_context(tc.psum_pool(name="sums_pool", bufs=2 * PAIRS))

        x_tiles = {}

        def load_chunk(c):
            for h in range(PAIRS):
                x_tiles[c, h] = x_pool.tile([P, 2 * K], BF16, name="x_rows")
                nc.sync.dma_start(out=x_tiles[c, h][:], in_=x_pairs[c, h])

        def turn_row_tile(row_words, grouped_words):
            turned = turned_pool.tile([P, WORDS], F32, name="turned")
            for b in range(BLOCKS):
                cols = slice(b * P, (b + 1) * P)
                nc.tensor.transpose(out=turned[:, cols], in_=row_words[:, cols], identity=identity[:])
            nc.scalar.copy(
                out=grouped_words,
                in_=turned[:].rearrange("p (g u r) -> p g r u", g=PASSES, u=2),
            )

        identity = const.tile([P, P], F32, name="identity")
        make_identity(nc, identity[:])

        bias_rows = const.tile([P, BOTH], BF16, name="bias_rows")
        nc.vector.memset(bias_rows[:], 0.0)
        nc.scalar.dma_start(out=bias_rows[0:1, 0:QD], in_=bk.rearrange("(o q) -> o q", o=1))
        nc.scalar.dma_start(out=bias_rows[0:1, QD:BOTH], in_=bv.rearrange("(o q) -> o q", o=1))
        ones = const.tile([P, P], BF16, name="ones")
        nc.vector.memset(ones[:], 1.0)

        load_chunk(0)
        w_rows = const.tile([P, 2 * K], BF16, name="w_rows")
        nc.sync.dma_start(out=w_rows[:, 0:K], in_=Wk)
        nc.sync.dma_start(out=w_rows[:, K : 2 * K], in_=Wv)
        for c in range(1, AHEAD):
            load_chunk(c)

        grouped_tiles = {}
        code_tiles = {}
        scale_tiles = {}
        sum_tiles = {}
        biased_tiles = {}

        def turn_chunk(c):
            grouped_tiles[c] = mx_pool.tile([P, TILES * K], BF16, name="grouped", align_bytes=64)
            code_tiles[c] = mx_pool.tile([P, TILES * K // PACK], U32, name="codes", align_bytes=64)
            scale_tiles[c] = mx_pool.tile([P, TILES * K // PACK], U8, name="scales", align_bytes=64)
            grouped_words = grouped_tiles[c][:].bitcast(F32)
            for j in range(TILES):
                h, i = divmod(j, 2)
                turn_row_tile(
                    x_tiles[c, h][:].bitcast(F32)[:, i * WORDS : (i + 1) * WORDS],
                    grouped_words[:, j * WORDS : (j + 1) * WORDS].rearrange("p (g r u) -> p g r u", g=PASSES, u=2),
                )

        def quantise_pair(c, h):
            width = 2 * K // PACK
            nc.vector.quantize_mx(
                out=code_tiles[c][:, h * width : (h + 1) * width].bitcast(FP8X4),
                scales=scale_tiles[c][:, h * width : (h + 1) * width],
                in_=grouped_tiles[c][:, h * width * PACK : (h + 1) * width * PACK],
            )

        def multiply_chunk(c):
            for h in range(PAIRS):
                sums = sums_pool.tile([P, 2 * BOTH], F32, name="sums")
                sum_tiles[c, h] = sums
                for i in range(2):
                    for g in range(PASSES):
                        first = ((2 * h + i) * PASSES + g) * P
                        nc.tensor.matmul_mx(
                            out=sums[:, i * BOTH : (i + 1) * BOTH],
                            lhsT=code_tiles[c][:, first : first + P].bitcast(FP8X4),
                            lhsT_scale=scale_tiles[c][:, first : first + P],
                            rhs=w_codes[:, g * BOTH : (g + 1) * BOTH].bitcast(FP8X4),
                            rhs_scale=w_scales[:, g * BOTH : (g + 1) * BOTH],
                            start=(g == 0),
                            stop=(g == PASSES - 1),
                        )

        def add_bias_pair(c, h):
            if h == 0:
                biased_tiles[c] = mx_pool.tile([P, TILES, BOTH], F32, name="biased")
            nc.vector.tensor_tensor(
                out=biased_tiles[c][:, 2 * h : 2 * h + 2, :],
                in0=sum_tiles[c, h][:].rearrange("p (i n) -> p i n", i=2),
                in1=bias[:].unsqueeze(1).to_broadcast([P, 2, BOTH]),
                op=ADD,
            )

        def finish_chunk(c):
            kv = out_pool.tile([P, TILES, QD], F32, name="kv")
            nc.gpsimd.tensor_tensor(
                out=kv[:], in0=biased_tiles[c][:, :, 0:QD], in1=biased_tiles[c][:, :, QD:BOTH], op=MULT
            )
            nc.sync.dma_start(out=out_chunks[c], in_=kv[:].rearrange("p j q -> p (j q)"))

        turn_chunk(0)
        for h in range(PAIRS):
            quantise_pair(0, h)

        w_grouped = const.tile([P, PASSES * BOTH * PACK], BF16, name="w_grouped", align_bytes=64)
        w_codes = const.tile([P, PASSES * BOTH], U32, name="w_codes", align_bytes=64)
        w_scales = const.tile([P, PASSES * BOTH], U8, name="w_scales", align_bytes=64)
        w_words = w_rows[:].bitcast(F32)
        w_grouped_words = w_grouped[:].bitcast(F32).rearrange("p (g v r u) -> p g v r u", g=PASSES, v=2, u=2)
        for v in range(2):
            turn_row_tile(w_words[:, v * WORDS : (v + 1) * WORDS], w_grouped_words[:, :, v, :, :])
        nc.vector.quantize_mx(out=w_codes[:].bitcast(FP8X4), scales=w_scales[:], in_=w_grouped[:])

        bias_sums = sums_pool.tile([P, 2 * BOTH], F32, name="sums")
        nc.tensor.matmul(out=bias_sums[:, 0:BOTH], lhsT=ones[:], rhs=bias_rows[:], start=True, stop=True)
        bias = const.tile([P, BOTH], F32, name="bias")
        nc.vector.tensor_copy(out=bias[:], in_=bias_sums[:, 0:BOTH])

        for c in range(1, CHUNKS + 1):
            if c - 1 + AHEAD < CHUNKS:
                load_chunk(c - 1 + AHEAD)
            if c < CHUNKS:
                turn_chunk(c)
            multiply_chunk(c - 1)
            for h in range(PAIRS):
                if c < CHUNKS:
                    quantise_pair(c, h)
                add_bias_pair(c - 1, h)
            finish_chunk(c - 1)
